import numpy as np
import ml_dtypes


def mxq(x, axis, fmt="e4m3"):
    dtype, down = {"e4m3": (ml_dtypes.float8_e4m3fn, 7), "e5m2": (ml_dtypes.float8_e5m2, 14)}[fmt]
    v = np.moveaxis(np.asarray(x, np.float32).astype(ml_dtypes.bfloat16).astype(np.float64), axis, -1)
    blocks = v.reshape(v.shape[:-1] + (-1, 32))
    amax = np.abs(blocks).max(-1, keepdims=True)
    byte = np.maximum(np.where(amax > 0, np.frexp(amax)[1] - 1 + 127, 0) - down, 1)
    scale = np.exp2(byte - 127.0)
    codes = (blocks / scale).astype(np.float32).astype(dtype).astype(np.float64)
    return np.moveaxis((codes * scale).reshape(v.shape), -1, axis)


WIDE = False


def mx_kscale(k):
    if not WIDE:
        return np.ones(k)
    levels = np.array([10, -10, 5, -5, 0])
    if k % 512:
        return np.exp2(np.random.permutation(np.resize(levels, k // 32))).repeat(32)
    a = np.empty((k // 512, 16))
    for p in range(k // 512):
        a[p, :8] = np.random.permutation(np.resize(levels, 8))
        for g in range(8):
            far = levels[np.abs(levels - a[p, g]) >= 10]
            a[p, g + 8] = far[np.random.randint(len(far))]
    return np.exp2(a.ravel()).repeat(32)


BF16 = ml_dtypes.bfloat16


def bf(x):
    return np.asarray(x, np.float32).astype(BF16)


def f64(x):
    return np.asarray(x).astype(np.float64)


B, S, D, DM, DK = 2, 512, 1024, 1024, 64
LN_EPS = 1e-5


def setup_inputs():
    s = mx_kscale(DM)
    return {
        "h_attn": bf(np.random.standard_normal((B, S, DM)) * 0.3 * s),
        "Wo": bf(np.random.standard_normal((DM, D)) * 3.0 / np.sqrt(DM) / s[:, None]),
        "bo": bf(np.random.standard_normal((B, S, D)) * 0.5 + np.random.uniform(0.25, 0.75, (B, 1, 1))),
        "x": bf(np.random.standard_normal((B, S, D))),
        "gamma": bf(1.0 + 0.1 * np.random.standard_normal((S, D))),
        "beta": bf(0.1 * np.random.standard_normal((S, D))),
    }


def reference(h_attn, Wo, bo, x, gamma, beta):
    o = (mxq(f64(h_attn), 2, "e4m3") @ mxq(f64(Wo), 0, "e4m3")) + f64(bo)
    o = o + f64(x)
    mu = o.mean(axis=(-2, -1), keepdims=True)
    var = np.square(o - mu).mean(axis=(-2, -1), keepdims=True)
    return (o - mu) / np.sqrt(var + LN_EPS) * f64(gamma) + f64(beta)

@@ -1,0 +1,281 @@
+from contextlib import ExitStack
+
+import concourse.mybir as mybir
+from concourse.masks import make_identity
+
+F32 = mybir.dt.float32
+BF16 = mybir.dt.bfloat16
+U32 = mybir.dt.uint32
+U8 = mybir.dt.uint8
+FP8X4 = mybir.dt.float8_e4m3fn_x4
+ALU = mybir.AluOpType
+ACT = mybir.ActivationFunctionType
+
+P = 128
+BATCH = 2
+SEQ = 512
+K = 1024
+N = 1024
+LN_EPS = 1e-5
+
+PACK = 4
+K_PASS = P * PACK
+PASSES = K // K_PASS
+HALVES = 2
+N_BLOCK = 512
+N_BLOCKS = N // N_BLOCK
+TILES = SEQ // P
+RUN = 4
+
+VECTOR_COLS = 672
+
+FLOPS = 2 * BATCH * SEQ * K * N
+
+
+def tile_multiheadattn_pb_kernel(tc, h_attn, Wo, bo, x, gamma, beta, out):
+    nc = tc.nc
+    with ExitStack() as ctx:
+        const = ctx.enter_context(tc.tile_pool(name="const", bufs=1))
+        keep = ctx.enter_context(tc.tile_pool(name="keep", bufs=1))
+        scratch = ctx.enter_context(tc.tile_pool(name="scratch", bufs=2))
+        psum_t = ctx.enter_context(tc.psum_pool(name="psum_t", bufs=3))
+        psum_acc = ctx.enter_context(tc.psum_pool(name="psum_acc", bufs=4))
+        psum_stat = ctx.enter_context(tc.psum_pool(name="psum_stat", bufs=1))
+        ctx.enter_context(tc.manual_schedule())
+
+        ident = const.tile([P, P], F32)
+        make_identity(nc, ident[:])
+        mean_w = const.tile([P, P], F32)
+        nc.vector.memset(mean_w[:], 1.0 / (SEQ * N))
+        eps = const.tile([P, 1], F32)
+        nc.vector.memset(eps[:], LN_EPS)
+        warm = const.tile([P, 1], F32)
+        nc.scalar.activation(out=warm[:], in_=eps[:], func=ACT.Sqrt)
+
+        h_view = h_attn.rearrange("b (p j) k -> b p j k", j=TILES)
+        bo_view = bo.rearrange("b (p j) n -> b p j n", j=TILES)
+        x_view = x.rearrange("b (p j) n -> b p j n", j=TILES)
+        gamma_view = gamma.rearrange("(p j) n -> p j n", j=TILES)
+        beta_view = beta.rearrange("(p j) n -> p j n", j=TILES)
+        out_view = out.rearrange("b (p j) n -> b p j n", j=TILES)
+
+        wo_raw = [keep.tile([P, PACK, N], BF16, name="wo_raw%d" % g) for g in range(PASSES)]
+        h_raw = [keep.tile([P, TILES, K], BF16, name="h_raw%d" % b) for b in range(BATCH)]
+        bo_sb = [keep.tile([P, TILES, N], BF16, name="bo_sb%d" % b) for b in range(BATCH)]
+        x_sb = [keep.tile([P, TILES, N], BF16, name="x_sb%d" % b) for b in range(BATCH)]
+        gamma_sb = keep.tile([P, TILES, N], BF16)
+        beta_sb = keep.tile([P, TILES, N], BF16)
+
+        def load_in_halves(pairs):
+            half = TILES // 2
+            for first in (0, half):
+                for dst, src in pairs:
+                    nc.sync.dma_start(
+                        out=dst[:, first : first + half, :], in_=src[:, first : first + half, :]
+                    )
+
+        def load_wo():
+            for g in range(PASSES):
+                rows = Wo[K_PASS * g : K_PASS * (g + 1), :].rearrange("(q t) c -> q t c", t=PACK)
+                for u in range(HALVES):
+                    pair = slice(2 * u, 2 * u + 2)
+                    nc.sync.dma_start(out=wo_raw[g][:, pair, :], in_=rows[:, pair, :])
+
+        load_wo()
+        load_in_halves([(h_raw[0], h_view[0])])
+        load_in_halves([(h_raw[1], h_view[1])])
+        load_in_halves([(bo_sb[0], bo_view[0]), (x_sb[0], x_view[0])])
+        load_in_halves([(bo_sb[1], bo_view[1]), (x_sb[1], x_view[1])])
+        load_in_halves([(gamma_sb, gamma_view)])
+        load_in_halves([(beta_sb, beta_view)])
+
+        wo_codes = [
+            keep.tile([P, N], U32, name="wo_codes%d" % g, align_bytes=64) for g in range(PASSES)
+        ]
+        wo_scales = [
+            keep.tile([P, N], U8, name="wo_scales%d" % g, align_bytes=64) for g in range(PASSES)
+        ]
+        o_sb = [keep.tile([P, TILES, N], F32, name="o_sb%d" % b) for b in range(BATCH)]
+        out_sb = [keep.tile([P, TILES, N], F32, name="out_sb%d" % b) for b in range(BATCH)]
+        h_codes = [
+            [
+                keep.tile([P, PASSES * P], U32, name="h_codes%d_%d" % (b, j), align_bytes=64)
+                for j in range(TILES)
+            ]
+            for b in range(BATCH)
+        ]
+        h_scales = [
+            [
+                keep.tile([P, PASSES * P], U8, name="h_scales%d_%d" % (b, j), align_bytes=64)
+                for j in range(TILES)
+            ]
+            for b in range(BATCH)
+        ]
+        chunk_sums = [
+            keep.tile([P, TILES * N_BLOCKS], F32, name="chunk_sums%d" % b) for b in range(BATCH)
+        ]
+        square_sums = [keep.tile([P, 1], F32, name="square_sums%d" % b) for b in range(BATCH)]
+        neg_mean = [keep.tile([P, 1], F32, name="neg_mean%d" % b) for b in range(BATCH)]
+        rstd = [keep.tile([P, 1], F32, name="rstd%d" % b) for b in range(BATCH)]
+
+        def quantise_wo():
+            wo_grouped = []
+            for g in range(PASSES):
+                grouped = keep.tile([P, N, PACK], BF16, name="wo_grouped%d" % g, align_bytes=64)
+                for copy, cols in (
+                    (nc.vector.tensor_copy, slice(0, VECTOR_COLS)),
+                    (nc.scalar.copy, slice(VECTOR_COLS, N)),
+                ):
+                    copy(
+                        out=grouped[:, cols, :].rearrange("p (c i) t -> p c t i", i=RUN),
+                        in_=wo_raw[g][:, :, cols].rearrange("p t (c i) -> p c t i", i=RUN),
+                    )
+                wo_grouped.append(grouped)
+            for n in range(N_BLOCKS):
+                cols = slice(N_BLOCK * n, N_BLOCK * (n + 1))
+                for g in range(PASSES):
+                    nc.vector.quantize_mx(
+                        out=wo_codes[g][:, cols].bitcast(FP8X4),
+                        scales=wo_scales[g][:, cols],
+                        in_=wo_grouped[g][:, cols, :].rearrange("p c t -> p (c t)"),
+                    )
+
+        def quantise_h(b):
+            for j in range(TILES):
+                words = h_raw[b][:, j, :].bitcast(F32)
+                turned = psum_t.tile([P, PASSES, HALVES, P], F32, name="turned")
+                for g in range(PASSES):
+                    for u in range(HALVES):
+                        first = HALVES * P * g
+                        nc.tensor.transpose(
+                            turned[:, g, u, :],
+                            words[:, first + u : first + HALVES * P : HALVES],
+                            ident[:],
+                        )
+                grouped = keep.tile(
+                    [P, PASSES, P, PACK], BF16, name="h_grouped%d_%d" % (b, j), align_bytes=64
+                )
+                nc.scalar.copy(
+                    out=grouped[:].bitcast(F32),
+                    in_=turned[:].rearrange("p g u r -> p g r u"),
+                )
+                nc.vector.quantize_mx(
+                    out=h_codes[b][j][:].bitcast(FP8X4),
+                    scales=h_scales[b][j][:],
+                    in_=grouped[:].rearrange("p g r t -> p (g r t)"),
+                )
+
+        def add_bias_and_residual(engine, b, tiles):
+            engine.tensor_tensor(
+                out=o_sb[b][:, tiles, :],
+                in0=bo_sb[b][:, tiles, :],
+                in1=x_sb[b][:, tiles, :],
+                op=ALU.add,
+            )
+
+        def project(b, tiles):
+            for j in tiles:
+                for n in range(N_BLOCKS):
+                    cols = slice(N_BLOCK * n, N_BLOCK * (n + 1))
+                    acc = psum_acc.tile([P, N_BLOCK], F32, name="acc")
+                    for g in range(PASSES):
+                        tokens = slice(P * g, P * (g + 1))
+                        nc.tensor.matmul_mx(
+                            out=acc[:],
+                            lhsT=h_codes[b][j][:, tokens].bitcast(FP8X4),
+                            lhsT_scale=h_scales[b][j][:, tokens],
+                            rhs=wo_codes[g][:, cols].bitcast(FP8X4),
+                            rhs_scale=wo_scales[g][:, cols],
+                            start=(g == 0),
+                            stop=(g == PASSES - 1),
+                        )
+                    chunk = N_BLOCKS * j + n
+                    nc.vector.scalar_tensor_tensor(
+                        out=o_sb[b][:, j, cols],
+                        in0=acc[:],
+                        scalar=1.0,
+                        in1=o_sb[b][:, j, cols],
+                        op0=ALU.mult,
+                        op1=ALU.add,
+                        accum_out=chunk_sums[b][:, chunk : chunk + 1],
+                    )
+
+        def find_mean(b):
+            chunks = TILES * N_BLOCKS
+            chunk_means = psum_stat.tile([P, chunks], F32, name="chunk_means", tag="stat")
+            nc.tensor.matmul(
+                out=chunk_means[:], lhsT=mean_w[:], rhs=chunk_sums[b][:], start=True, stop=True
+            )
+            unread = scratch.tile([P, chunks], F32, name="unread")
+            nc.scalar.activation(
+                out=unread[:],
+                in_=chunk_means[:],
+                func=ACT.Copy,
+                scale=-1.0,
+                accum_out=neg_mean[b][:],
+            )
+
+        def sum_squares(b):
+            squares = scratch.tile([P, TILES, N], BF16, name="squares")
+            nc.scalar.activation(
+                out=squares[:],
+                in_=o_sb[b][:],
+                func=ACT.Square,
+                bias=neg_mean[b][:],
+                scale=1.0,
+                accum_out=square_sums[b][:],
+            )
+
+        def find_rstd(b):
+            var = psum_stat.tile([P, 1], F32, name="var", tag="stat")
+            nc.tensor.matmul(
+                out=var[:], lhsT=mean_w[:], rhs=square_sums[b][:], start=True, stop=True
+            )
+            std = scratch.tile([P, 1], F32, name="std")
+            nc.scalar.activation(out=std[:], in_=var[:], func=ACT.Sqrt, bias=eps[:], scale=1.0)
+            nc.vector.reciprocal(out=rstd[b][:], in_=std[:])
+
+        def centre_and_gain(b):
+            nc.vector.scalar_tensor_tensor(
+                out=out_sb[b][:],
+                in0=o_sb[b][:],
+                scalar=neg_mean[b][:],
+                in1=gamma_sb[:],
+                op0=ALU.add,
+                op1=ALU.mult,
+            )
+
+        def scale_shift_store(b):
+            for j in range(TILES):
+                nc.vector.scalar_tensor_tensor(
+                    out=out_sb[b][:, j, :],
+                    in0=out_sb[b][:, j, :],
+                    scalar=rstd[b][:],
+                    in1=beta_sb[:, j, :],
+                    op0=ALU.mult,
+                    op1=ALU.add,
+                )
+                nc.sync.dma_start(out=out_view[b, :, j, :], in_=out_sb[b][:, j, :])
+
+        quantise_wo()
+        quantise_h(0)
+        add_bias_and_residual(nc.vector, 0, slice(0, TILES // 2))
+        quantise_h(1)
+        add_bias_and_residual(nc.vector, 0, slice(TILES // 2, TILES))
+
+        for j in range(TILES):
+            add_bias_and_residual(nc.gpsimd, 1, slice(j, j + 1))
+        project(0, range(TILES))
+        project(1, range(1))
+        find_mean(0)
+        project(1, range(1, TILES))
+
+        sum_squares(0)
+        find_mean(1)
+        centre_and_gain(0)
+        find_rstd(0)
+        scale_shift_store(0)
+        sum_squares(1)
+        centre_and_gain(1)
+        find_rstd(1)
+        scale_shift_store(1)

@@ -27,7 +27,7 @@ N_BLOCKS = N // N_BLOCK
 TILES = SEQ // P
 RUN = 4
 
-VECTOR_COLS = 672
+VECTOR_COLS = 256
 
 FLOPS = 2 * BATCH * SEQ * K * N
 
@@ -38,15 +38,21 @@ def tile_multiheadattn_pb_kernel(tc, h_attn, Wo, bo, x, gamma, beta, out):
         const = ctx.enter_context(tc.tile_pool(name="const", bufs=1))
         keep = ctx.enter_context(tc.tile_pool(name="keep", bufs=1))
         scratch = ctx.enter_context(tc.tile_pool(name="scratch", bufs=2))
-        psum_t = ctx.enter_context(tc.psum_pool(name="psum_t", bufs=3))
+        psum_work = ctx.enter_context(tc.psum_pool(name="psum_work", bufs=3))
         psum_acc = ctx.enter_context(tc.psum_pool(name="psum_acc", bufs=4))
         psum_stat = ctx.enter_context(tc.psum_pool(name="psum_stat", bufs=1))
         ctx.enter_context(tc.manual_schedule())
 
         ident = const.tile([P, P], F32)
         make_identity(nc, ident[:])
+        ident16 = const.tile([P, P], BF16)
+        make_identity(nc, ident16[:])
         mean_w = const.tile([P, P], F32)
         nc.vector.memset(mean_w[:], 1.0 / (SEQ * N))
+        within_w = const.tile([P, P], F32)
+        nc.vector.memset(within_w[:], 1.0 / (SEQ * N * N_BLOCK * N_BLOCK))
+        between_w = const.tile([P, P], F32)
+        nc.vector.memset(between_w[:], N_BLOCK / (SEQ * N))
         eps = const.tile([P, 1], F32)
         nc.vector.memset(eps[:], LN_EPS)
         warm = const.tile([P, 1], F32)
@@ -59,35 +65,43 @@ def tile_multiheadattn_pb_kernel(tc, h_attn, Wo, bo, x, gamma, beta, out):
         beta_view = beta.rearrange("(p j) n -> p j n", j=TILES)
         out_view = out.rearrange("b (p j) n -> b p j n", j=TILES)
 
-        wo_raw = [keep.tile([P, PACK, N], BF16, name="wo_raw%d" % g) for g in range(PASSES)]
+        wo_raw = [
+            [
+                keep.tile([P, PACK, N_BLOCK], BF16, name="wo_raw%d_%d" % (g, n))
+                for n in range(N_BLOCKS)
+            ]
+            for g in range(PASSES)
+        ]
         h_raw = [keep.tile([P, TILES, K], BF16, name="h_raw%d" % b) for b in range(BATCH)]
         bo_sb = [keep.tile([P, TILES, N], BF16, name="bo_sb%d" % b) for b in range(BATCH)]
         x_sb = [keep.tile([P, TILES, N], BF16, name="x_sb%d" % b) for b in range(BATCH)]
         gamma_sb = keep.tile([P, TILES, N], BF16)
         beta_sb = keep.tile([P, TILES, N], BF16)
 
-        def load_in_halves(pairs):
-            half = TILES // 2
-            for first in (0, half):
-                for dst, src in pairs:
-                    nc.sync.dma_start(
-                        out=dst[:, first : first + half, :], in_=src[:, first : first + half, :]
-                    )
+        def load_half(pairs, first):
+            for dst, src in pairs:
+                nc.sync.dma_start(out=dst[:, first : first + 2, :], in_=src[:, first : first + 2, :])
 
-        def load_wo():
+        def load_wo(g, n):
+            nc.sync.dma_start(
+                out=wo_raw[g][n][:],
+                in_=Wo[
+                    K_PASS * g : K_PASS * (g + 1), N_BLOCK * n : N_BLOCK * (n + 1)
+                ].rearrange("(q t) c -> q t c", t=PACK),
+            )
+
+        for n in range(N_BLOCKS):
             for g in range(PASSES):
-                rows = Wo[K_PASS * g : K_PASS * (g + 1), :].rearrange("(q t) c -> q t c", t=PACK)
-                for u in range(HALVES):
-                    pair = slice(2 * u, 2 * u + 2)
-                    nc.sync.dma_start(out=wo_raw[g][:, pair, :], in_=rows[:, pair, :])
-
-        load_wo()
-        load_in_halves([(h_raw[0], h_view[0])])
-        load_in_halves([(h_raw[1], h_view[1])])
-        load_in_halves([(bo_sb[0], bo_view[0]), (x_sb[0], x_view[0])])
-        load_in_halves([(bo_sb[1], bo_view[1]), (x_sb[1], x_view[1])])
-        load_in_halves([(gamma_sb, gamma_view)])
-        load_in_halves([(beta_sb, beta_view)])
+                load_wo(g, n)
+        load_half([(h_raw[0], h_view[0])], 0)
+        load_half([(h_raw[0], h_view[0])], 2)
+        load_half([(bo_sb[0], bo_view[0]), (x_sb[0], x_view[0])], 0)
+        load_half([(bo_sb[0], bo_view[0]), (x_sb[0], x_view[0])], 2)
+        nc.sync.dma_start(out=h_raw[1][:], in_=h_view[1])
+        load_half([(bo_sb[1], bo_view[1]), (x_sb[1], x_view[1])], 0)
+        load_half([(bo_sb[1], bo_view[1]), (x_sb[1], x_view[1])], 2)
+        nc.sync.dma_start(out=gamma_sb[:], in_=gamma_view)
+        nc.sync.dma_start(out=beta_sb[:], in_=beta_view)
 
         wo_codes = [
             keep.tile([P, N], U32, name="wo_codes%d" % g, align_bytes=64) for g in range(PASSES)
@@ -114,168 +128,342 @@ def tile_multiheadattn_pb_kernel(tc, h_attn, Wo, bo, x, gamma, beta, out):
         chunk_sums = [
             keep.tile([P, TILES * N_BLOCKS], F32, name="chunk_sums%d" % b) for b in range(BATCH)
         ]
-        square_sums = [keep.tile([P, 1], F32, name="square_sums%d" % b) for b in range(BATCH)]
+        within = [keep.tile([P, TILES * N_BLOCKS], F32, name="within%d" % b) for b in range(BATCH)]
         neg_mean = [keep.tile([P, 1], F32, name="neg_mean%d" % b) for b in range(BATCH)]
+        std = [keep.tile([P, 1], F32, name="std%d" % b) for b in range(BATCH)]
         rstd = [keep.tile([P, 1], F32, name="rstd%d" % b) for b in range(BATCH)]
+        shift = [keep.tile([P, 1], F32, name="shift%d" % b) for b in range(BATCH)]
 
-        def quantise_wo():
-            wo_grouped = []
-            for g in range(PASSES):
-                grouped = keep.tile([P, N, PACK], BF16, name="wo_grouped%d" % g, align_bytes=64)
-                for copy, cols in (
-                    (nc.vector.tensor_copy, slice(0, VECTOR_COLS)),
-                    (nc.scalar.copy, slice(VECTOR_COLS, N)),
-                ):
-                    copy(
-                        out=grouped[:, cols, :].rearrange("p (c i) t -> p c t i", i=RUN),
-                        in_=wo_raw[g][:, :, cols].rearrange("p t (c i) -> p c t i", i=RUN),
-                    )
-                wo_grouped.append(grouped)
-            for n in range(N_BLOCKS):
-                cols = slice(N_BLOCK * n, N_BLOCK * (n + 1))
-                for g in range(PASSES):
-                    nc.vector.quantize_mx(
-                        out=wo_codes[g][:, cols].bitcast(FP8X4),
-                        scales=wo_scales[g][:, cols],
-                        in_=wo_grouped[g][:, cols, :].rearrange("p c t -> p (c t)"),
-                    )
-
-        def quantise_h(b):
-            for j in range(TILES):
-                words = h_raw[b][:, j, :].bitcast(F32)
-                turned = psum_t.tile([P, PASSES, HALVES, P], F32, name="turned")
-                for g in range(PASSES):
-                    for u in range(HALVES):
-                        first = HALVES * P * g
-                        nc.tensor.transpose(
-                            turned[:, g, u, :],
-                            words[:, first + u : first + HALVES * P : HALVES],
-                            ident[:],
-                        )
-                grouped = keep.tile(
-                    [P, PASSES, P, PACK], BF16, name="h_grouped%d_%d" % (b, j), align_bytes=64
+        def quantise_wo(g, n):
+            grouped = keep.tile(
+                [P, N_BLOCK, PACK], BF16, name="wo_grouped%d_%d" % (g, n), align_bytes=64
+            )
+            for copy, cols in (
+                (nc.vector.tensor_copy, slice(0, VECTOR_COLS)),
+                (nc.scalar.copy, slice(VECTOR_COLS, N_BLOCK)),
+            ):
+                copy(
+                    out=grouped[:, cols, :].rearrange("p (c i) t -> p c t i", i=RUN),
+                    in_=wo_raw[g][n][:, :, cols].rearrange("p t (c i) -> p c t i", i=RUN),
                 )
-                nc.scalar.copy(
-                    out=grouped[:].bitcast(F32),
-                    in_=turned[:].rearrange("p g u r -> p g r u"),
-                )
-                nc.vector.quantize_mx(
-                    out=h_codes[b][j][:].bitcast(FP8X4),
-                    scales=h_scales[b][j][:],
-                    in_=grouped[:].rearrange("p g r t -> p (g r t)"),
-                )
-
-        def add_bias_and_residual(engine, b, tiles):
-            engine.tensor_tensor(
-                out=o_sb[b][:, tiles, :],
-                in0=bo_sb[b][:, tiles, :],
-                in1=x_sb[b][:, tiles, :],
-                op=ALU.add,
+            cols = slice(N_BLOCK * n, N_BLOCK * (n + 1))
+            nc.vector.quantize_mx(
+                out=wo_codes[g][:, cols].bitcast(FP8X4),
+                scales=wo_scales[g][:, cols],
+                in_=grouped[:].rearrange("p c t -> p (c t)"),
             )
 
-        def project(b, tiles):
-            for j in tiles:
-                for n in range(N_BLOCKS):
-                    cols = slice(N_BLOCK * n, N_BLOCK * (n + 1))
-                    acc = psum_acc.tile([P, N_BLOCK], F32, name="acc")
-                    for g in range(PASSES):
-                        tokens = slice(P * g, P * (g + 1))
-                        nc.tensor.matmul_mx(
-                            out=acc[:],
-                            lhsT=h_codes[b][j][:, tokens].bitcast(FP8X4),
-                            lhsT_scale=h_scales[b][j][:, tokens],
-                            rhs=wo_codes[g][:, cols].bitcast(FP8X4),
-                            rhs_scale=wo_scales[g][:, cols],
-                            start=(g == 0),
-                            stop=(g == PASSES - 1),
-                        )
-                    chunk = N_BLOCKS * j + n
-                    nc.vector.scalar_tensor_tensor(
-                        out=o_sb[b][:, j, cols],
-                        in0=acc[:],
-                        scalar=1.0,
-                        in1=o_sb[b][:, j, cols],
-                        op0=ALU.mult,
-                        op1=ALU.add,
-                        accum_out=chunk_sums[b][:, chunk : chunk + 1],
+        h_turned = {}
+        h_grouped = {}
+
+        def turn_h(b, j):
+            words = h_raw[b][:, j, :].bitcast(F32)
+            turned = psum_work.tile([P, PASSES, HALVES, P], F32, name="turned", tag="work")
+            for g in range(PASSES):
+                for u in range(HALVES):
+                    first = HALVES * P * g
+                    nc.tensor.transpose(
+                        turned[:, g, u, :],
+                        words[:, first + u : first + HALVES * P : HALVES],
+                        ident[:],
                     )
+            h_turned[b, j] = turned
+
+        def group_h(copy, b, j):
+            grouped = keep.tile(
+                [P, PASSES, P, PACK], BF16, name="h_grouped%d_%d" % (b, j), align_bytes=64
+            )
+            copy(
+                out=grouped[:].bitcast(F32),
+                in_=h_turned[b, j][:].rearrange("p g u r -> p g r u"),
+            )
+            h_grouped[b, j] = grouped
+
+        def quantise_h(b, j):
+            nc.vector.quantize_mx(
+                out=h_codes[b][j][:].bitcast(FP8X4),
+                scales=h_scales[b][j][:],
+                in_=h_grouped[b, j][:].rearrange("p g r t -> p (g r t)"),
+            )
+
+        def place(chunk):
+            j, n = divmod(chunk, N_BLOCKS)
+            return j, slice(N_BLOCK * n, N_BLOCK * (n + 1))
+
+        def add_on(engine, b, some):
+            for chunk in some:
+                j, cols = place(chunk)
+                engine.tensor_tensor(
+                    out=o_sb[b][:, j, cols],
+                    in0=bo_sb[b][:, j, cols],
+                    in1=x_sb[b][:, j, cols],
+                    op=ALU.add,
+                )
+
+        boths = {}
+
+        def add_on_tensor(b, some):
+            for chunk in some:
+                j, cols = place(chunk)
+                both = psum_work.tile([P, N_BLOCK], F32, name="both", tag="work")
+                boths[b, chunk] = both
+                nc.tensor.matmul(
+                    out=both[:], lhsT=ident16[:], rhs=bo_sb[b][:, j, cols], start=True, stop=False
+                )
+                nc.tensor.matmul(
+                    out=both[:], lhsT=ident16[:], rhs=x_sb[b][:, j, cols], start=False, stop=True
+                )
+
+        def bring_out(b, some):
+            for chunk in some:
+                j, cols = place(chunk)
+                nc.scalar.copy(out=o_sb[b][:, j, cols], in_=boths[b, chunk][:])
+
+        accs = {}
+
+        def multiply(b, some):
+            for chunk in some:
+                j, cols = place(chunk)
+                acc = psum_acc.tile([P, N_BLOCK], F32, name="acc")
+                accs[b, chunk] = acc
+                for g in range(PASSES):
+                    tokens = slice(P * g, P * (g + 1))
+                    nc.tensor.matmul_mx(
+                        out=acc[:],
+                        lhsT=h_codes[b][j][:, tokens].bitcast(FP8X4),
+                        lhsT_scale=h_scales[b][j][:, tokens],
+                        rhs=wo_codes[g][:, cols].bitcast(FP8X4),
+                        rhs_scale=wo_scales[g][:, cols],
+                        start=(g == 0),
+                        stop=(g == PASSES - 1),
+                    )
+
+        def collect(b, some):
+            for chunk in some:
+                j, cols = place(chunk)
+                nc.vector.scalar_tensor_tensor(
+                    out=o_sb[b][:, j, cols],
+                    in0=accs[b, chunk][:],
+                    scalar=1.0,
+                    in1=o_sb[b][:, j, cols],
+                    op0=ALU.mult,
+                    op1=ALU.add,
+                    accum_out=chunk_sums[b][:, chunk : chunk + 1],
+                )
+
+        chunks = TILES * N_BLOCKS
+
+        def square(b, some):
+            for chunk in some:
+                squares = scratch.tile([P, N_BLOCK], BF16, name="squares")
+                j, cols = place(chunk)
+                nc.scalar.activation(
+                    out=squares[:],
+                    in_=o_sb[b][:, j, cols],
+                    func=ACT.Square,
+                    bias=chunk_sums[b][:, chunk : chunk + 1],
+                    scale=-float(N_BLOCK),
+                    accum_out=within[b][:, chunk : chunk + 1],
+                )
+
+        chunk_means = {}
+        parts = {}
+
+        def add_sums_over_partitions(b):
+            chunk_means[b] = psum_stat.tile([P, chunks], F32, name="chunk_means", tag="stat")
+            nc.tensor.matmul(
+                out=chunk_means[b][:], lhsT=mean_w[:], rhs=chunk_sums[b][:], start=True, stop=True
+            )
+
+        between = [keep.tile([P, chunks], F32, name="between%d" % b) for b in range(BATCH)]
 
         def find_mean(b):
-            chunks = TILES * N_BLOCKS
-            chunk_means = psum_stat.tile([P, chunks], F32, name="chunk_means", tag="stat")
-            nc.tensor.matmul(
-                out=chunk_means[:], lhsT=mean_w[:], rhs=chunk_sums[b][:], start=True, stop=True
-            )
             unread = scratch.tile([P, chunks], F32, name="unread")
             nc.scalar.activation(
                 out=unread[:],
-                in_=chunk_means[:],
+                in_=chunk_means[b][:],
                 func=ACT.Copy,
                 scale=-1.0,
                 accum_out=neg_mean[b][:],
             )
-
-        def sum_squares(b):
-            squares = scratch.tile([P, TILES, N], BF16, name="squares")
             nc.scalar.activation(
-                out=squares[:],
-                in_=o_sb[b][:],
+                out=between[b][:],
+                in_=chunk_sums[b][:],
                 func=ACT.Square,
                 bias=neg_mean[b][:],
-                scale=1.0,
-                accum_out=square_sums[b][:],
+                scale=1.0 / N_BLOCK,
             )
+
+        def add_squares_over_partitions(b):
+            parts[b] = psum_stat.tile([P, chunks], F32, name="parts", tag="stat")
+            nc.tensor.matmul(
+                out=parts[b][:], lhsT=within_w[:], rhs=within[b][:], start=True, stop=False
+            )
+            nc.tensor.matmul(
+                out=parts[b][:], lhsT=between_w[:], rhs=between[b][:], start=False, stop=True
+            )
+
+        def find_std(b):
+            unread = scratch.tile([P, chunks], F32, name="unread")
+            var = scratch.tile([P, 1], F32, name="var")
+            nc.scalar.activation(out=unread[:], in_=parts[b][:], func=ACT.Copy, accum_out=var[:])
+            nc.scalar.activation(out=std[b][:], in_=var[:], func=ACT.Sqrt, bias=eps[:], scale=1.0)
 
         def find_rstd(b):
-            var = psum_stat.tile([P, 1], F32, name="var", tag="stat")
-            nc.tensor.matmul(
-                out=var[:], lhsT=mean_w[:], rhs=square_sums[b][:], start=True, stop=True
-            )
-            std = scratch.tile([P, 1], F32, name="std")
-            nc.scalar.activation(out=std[:], in_=var[:], func=ACT.Sqrt, bias=eps[:], scale=1.0)
-            nc.vector.reciprocal(out=rstd[b][:], in_=std[:])
-
-        def centre_and_gain(b):
-            nc.vector.scalar_tensor_tensor(
-                out=out_sb[b][:],
-                in0=o_sb[b][:],
-                scalar=neg_mean[b][:],
-                in1=gamma_sb[:],
-                op0=ALU.add,
-                op1=ALU.mult,
+            nc.vector.reciprocal(out=rstd[b][:], in_=std[b][:])
+            nc.scalar.activation(
+                out=shift[b][:], in_=neg_mean[b][:], func=ACT.Copy, scale=rstd[b][:]
             )
 
-        def scale_shift_store(b):
-            for j in range(TILES):
+        words = N_BLOCK // P
+        in_sbuf = {"gamma": gamma_sb, "beta": beta_sb}
+        in_psum = {}
+        turned = {}
+        turned_sb = {}
+
+        def turn(name, j):
+            turned[name, j] = psum_work.tile([P, words, P], F32, name="turned_once", tag="work")
+            for w in range(words):
+                nc.tensor.transpose(
+                    turned[name, j][:, w, :],
+                    in_sbuf[name][:, j, :].bitcast(F32)[:, P * w : P * (w + 1)],
+                    ident[:],
+                )
+
+        def copy_turned(name, j):
+            turned_sb[name, j] = keep.tile([P, words, P], F32, name="turned_%s%d" % (name, j))
+            nc.scalar.copy(out=turned_sb[name, j][:], in_=turned[name, j][:])
+
+        def turn_back(name, j):
+            back = psum_acc.tile([P, words, P], F32, name="turned_twice", tag="acc")
+            for w in range(words):
+                nc.tensor.transpose(back[:, w, :], turned_sb[name, j][:, w, :], ident[:])
+            in_psum[name, j] = back
+
+        def columns(name, chunk):
+            j, cols = place(chunk)
+            if (name, j) in in_psum:
+                back = in_psum[name, j][:].rearrange("p w r -> p (w r)")
+                return back.bitcast(BF16)[:, cols]
+            return in_sbuf[name][:, j, cols]
+
+        def finish_on_vector(b, some):
+            for chunk in some:
+                j, cols = place(chunk)
                 nc.vector.scalar_tensor_tensor(
-                    out=out_sb[b][:, j, :],
-                    in0=out_sb[b][:, j, :],
+                    out=out_sb[b][:, j, cols],
+                    in0=o_sb[b][:, j, cols],
+                    scalar=neg_mean[b][:],
+                    in1=columns("gamma", chunk),
+                    op0=ALU.add,
+                    op1=ALU.mult,
+                )
+            for chunk in some:
+                j, cols = place(chunk)
+                nc.vector.scalar_tensor_tensor(
+                    out=out_sb[b][:, j, cols],
+                    in0=out_sb[b][:, j, cols],
                     scalar=rstd[b][:],
-                    in1=beta_sb[:, j, :],
+                    in1=columns("beta", chunk),
                     op0=ALU.mult,
                     op1=ALU.add,
                 )
-                nc.sync.dma_start(out=out_view[b, :, j, :], in_=out_sb[b][:, j, :])
+                nc.sync.dma_start(out=out_view[b, :, j, cols], in_=out_sb[b][:, j, cols])
 
-        quantise_wo()
-        quantise_h(0)
-        add_bias_and_residual(nc.vector, 0, slice(0, TILES // 2))
-        quantise_h(1)
-        add_bias_and_residual(nc.vector, 0, slice(TILES // 2, TILES))
+        def normalise(b, some):
+            for chunk in some:
+                j, cols = place(chunk)
+                nc.scalar.activation(
+                    out=out_sb[b][:, j, cols],
+                    in_=o_sb[b][:, j, cols],
+                    func=ACT.Identity,
+                    bias=shift[b][:],
+                    scale=rstd[b][:],
+                )
 
+        def finish_on_gpsimd(b, some):
+            for chunk in some:
+                j, cols = place(chunk)
+                nc.vector.tensor_tensor(
+                    out=out_sb[b][:, j, cols],
+                    in0=out_sb[b][:, j, cols],
+                    in1=columns("gamma", chunk),
+                    op=ALU.mult,
+                )
+                nc.gpsimd.tensor_tensor(
+                    out=out_sb[b][:, j, cols],
+                    in0=out_sb[b][:, j, cols],
+                    in1=beta_sb[:, j, cols],
+                    op=ALU.add,
+                )
+                nc.sync.dma_start(out=out_view[b, :, j, cols], in_=out_sb[b][:, j, cols])
+
+        for n in range(N_BLOCKS):
+            for g in range(PASSES):
+                quantise_wo(g, n)
         for j in range(TILES):
-            add_bias_and_residual(nc.gpsimd, 1, slice(j, j + 1))
-        project(0, range(TILES))
-        project(1, range(1))
-        find_mean(0)
-        project(1, range(1, TILES))
+            turn_h(0, j)
+            group_h(nc.scalar.copy, 0, j)
+            quantise_h(0, j)
 
-        sum_squares(0)
-        find_mean(1)
-        centre_and_gain(0)
+        multiply(0, [0, 1])
+        add_on_tensor(0, [0, 1])
+        bring_out(0, [0, 1])
+        add_on(nc.gpsimd, 0, [2, 3])
+        multiply(0, [2, 3])
+        collect(0, [0, 1, 2])
+        add_on_tensor(0, [4])
+        square(0, [0])
+        bring_out(0, [4])
+        square(0, [1, 2])
+        add_on(nc.gpsimd, 0, [5, 6, 7])
+        multiply(0, [4, 5, 6])
+        collect(0, [3])
+        multiply(0, [7])
+        square(0, [3])
+        for j in range(TILES):
+            turn_h(1, j)
+            group_h(nc.scalar.copy, 1, j)
+            if j == 0:
+                collect(0, [4, 5, 6])
+        quantise_h(1, 0)
+        quantise_h(1, 1)
+        collect(0, [7])
+        quantise_h(1, 2)
+        quantise_h(1, 3)
+        multiply(1, [0])
+        add_on_tensor(1, [0])
+        bring_out(1, [0])
+        add_on(nc.gpsimd, 1, [1, 2, 3])
+        multiply(1, [1, 2, 3])
+        square(0, [4, 5, 6])
+        add_on_tensor(1, [4, 5])
+        bring_out(1, [4, 5])
+        square(0, [7])
+        collect(1, [0, 1, 2, 3])
+        add_on(nc.gpsimd, 1, [6, 7])
+        multiply(1, [4])
+        add_sums_over_partitions(0)
+        multiply(1, [5, 6])
+        find_mean(0)
+        square(1, [0, 1])
+        add_squares_over_partitions(0)
+        find_std(0)
+        multiply(1, [7])
+        collect(1, [4, 5, 6])
         find_rstd(0)
-        scale_shift_store(0)
-        sum_squares(1)
-        centre_and_gain(1)
+        collect(1, [7])
+        square(1, [2, 3, 4, 5, 6, 7])
+        finish_on_vector(0, [0, 1])
+        finish_on_vector(0, [2, 3])
+        add_sums_over_partitions(1)
+        find_mean(1)
+        add_squares_over_partitions(1)
+        find_std(1)
+        finish_on_vector(0, [4, 5])
+        finish_on_vector(0, [6, 7])
         find_rstd(1)
-        scale_shift_store(1)
+        finish_on_vector(1, [0, 1])
+        finish_on_vector(1, [2, 3])
+        finish_on_vector(1, [4, 5])
+        finish_on_vector(1, [6, 7])

@@ -27,7 +27,7 @@ N_BLOCKS = N // N_BLOCK
 TILES = SEQ // P
 RUN = 4
 
-VECTOR_COLS = 256
+VECTOR_COLS = 336
 
 FLOPS = 2 * BATCH * SEQ * K * N
 
@@ -66,11 +66,7 @@ def tile_multiheadattn_pb_kernel(tc, h_attn, Wo, bo, x, gamma, beta, out):
         out_view = out.rearrange("b (p j) n -> b p j n", j=TILES)
 
         wo_raw = [
-            [
-                keep.tile([P, PACK, N_BLOCK], BF16, name="wo_raw%d_%d" % (g, n))
-                for n in range(N_BLOCKS)
-            ]
-            for g in range(PASSES)
+            keep.tile([P, PACK, N], BF16, name="wo_raw%d" % g) for g in range(PASSES)
         ]
         h_raw = [keep.tile([P, TILES, K], BF16, name="h_raw%d" % b) for b in range(BATCH)]
         bo_sb = [keep.tile([P, TILES, N], BF16, name="bo_sb%d" % b) for b in range(BATCH)]
@@ -82,22 +78,20 @@ def tile_multiheadattn_pb_kernel(tc, h_attn, Wo, bo, x, gamma, beta, out):
             for dst, src in pairs:
                 nc.sync.dma_start(out=dst[:, first : first + 2, :], in_=src[:, first : first + 2, :])
 
-        def load_wo(g, n):
+        def load_wo(g):
             nc.sync.dma_start(
-                out=wo_raw[g][n][:],
-                in_=Wo[
-                    K_PASS * g : K_PASS * (g + 1), N_BLOCK * n : N_BLOCK * (n + 1)
-                ].rearrange("(q t) c -> q t c", t=PACK),
+                out=wo_raw[g][:],
+                in_=Wo[K_PASS * g : K_PASS * (g + 1), :].rearrange("(q t) c -> q t c", t=PACK),
             )
 
-        for n in range(N_BLOCKS):
-            for g in range(PASSES):
-                load_wo(g, n)
+        for g in range(PASSES):
+            load_wo(g)
         load_half([(h_raw[0], h_view[0])], 0)
         load_half([(h_raw[0], h_view[0])], 2)
+        load_half([(h_raw[1], h_view[1])], 0)
+        load_half([(h_raw[1], h_view[1])], 2)
         load_half([(bo_sb[0], bo_view[0]), (x_sb[0], x_view[0])], 0)
         load_half([(bo_sb[0], bo_view[0]), (x_sb[0], x_view[0])], 2)
-        nc.sync.dma_start(out=h_raw[1][:], in_=h_view[1])
         load_half([(bo_sb[1], bo_view[1]), (x_sb[1], x_view[1])], 0)
         load_half([(bo_sb[1], bo_view[1]), (x_sb[1], x_view[1])], 2)
         nc.sync.dma_start(out=gamma_sb[:], in_=gamma_view)
@@ -134,7 +128,9 @@ def tile_multiheadattn_pb_kernel(tc, h_attn, Wo, bo, x, gamma, beta, out):
         rstd = [keep.tile([P, 1], F32, name="rstd%d" % b) for b in range(BATCH)]
         shift = [keep.tile([P, 1], F32, name="shift%d" % b) for b in range(BATCH)]
 
-        def quantise_wo(g, n):
+        wo_grouped = {}
+
+        def group_wo(g, n):
             grouped = keep.tile(
                 [P, N_BLOCK, PACK], BF16, name="wo_grouped%d_%d" % (g, n), align_bytes=64
             )
@@ -142,15 +138,21 @@ def tile_multiheadattn_pb_kernel(tc, h_attn, Wo, bo, x, gamma, beta, out):
                 (nc.vector.tensor_copy, slice(0, VECTOR_COLS)),
                 (nc.scalar.copy, slice(VECTOR_COLS, N_BLOCK)),
             ):
+                first = N_BLOCK * n + cols.start
                 copy(
                     out=grouped[:, cols, :].rearrange("p (c i) t -> p c t i", i=RUN),
-                    in_=wo_raw[g][n][:, :, cols].rearrange("p t (c i) -> p c t i", i=RUN),
+                    in_=wo_raw[g][:, :, first : first + cols.stop - cols.start].rearrange(
+                        "p t (c i) -> p c t i", i=RUN
+                    ),
                 )
+            wo_grouped[g, n] = grouped
+
+        def quantise_wo(g, n):
             cols = slice(N_BLOCK * n, N_BLOCK * (n + 1))
             nc.vector.quantize_mx(
                 out=wo_codes[g][:, cols].bitcast(FP8X4),
                 scales=wo_scales[g][:, cols],
-                in_=grouped[:].rearrange("p c t -> p (c t)"),
+                in_=wo_grouped[g, n][:].rearrange("p c t -> p (c t)"),
             )
 
         h_turned = {}
@@ -334,8 +336,8 @@ def tile_multiheadattn_pb_kernel(tc, h_attn, Wo, bo, x, gamma, beta, out):
             turned_sb[name, j] = keep.tile([P, words, P], F32, name="turned_%s%d" % (name, j))
             nc.scalar.copy(out=turned_sb[name, j][:], in_=turned[name, j][:])
 
-        def turn_back(name, j):
-            back = psum_acc.tile([P, words, P], F32, name="turned_twice", tag="acc")
+        def turn_back(name, j, pool=psum_acc, tag="acc"):
+            back = pool.tile([P, words, P], F32, name="turned_twice", tag=tag)
             for w in range(words):
                 nc.tensor.transpose(back[:, w, :], turned_sb[name, j][:, w, :], ident[:])
             in_psum[name, j] = back
@@ -347,7 +349,7 @@ def tile_multiheadattn_pb_kernel(tc, h_attn, Wo, bo, x, gamma, beta, out):
                 return back.bitcast(BF16)[:, cols]
             return in_sbuf[name][:, j, cols]
 
-        def finish_on_vector(b, some):
+        def centre_and_gain(b, some):
             for chunk in some:
                 j, cols = place(chunk)
                 nc.vector.scalar_tensor_tensor(
@@ -358,6 +360,8 @@ def tile_multiheadattn_pb_kernel(tc, h_attn, Wo, bo, x, gamma, beta, out):
                     op0=ALU.add,
                     op1=ALU.mult,
                 )
+
+        def scale_shift_store(b, some):
             for chunk in some:
                 j, cols = place(chunk)
                 nc.vector.scalar_tensor_tensor(
@@ -369,6 +373,31 @@ def tile_multiheadattn_pb_kernel(tc, h_attn, Wo, bo, x, gamma, beta, out):
                     op1=ALU.add,
                 )
                 nc.sync.dma_start(out=out_view[b, :, j, cols], in_=out_sb[b][:, j, cols])
+
+        def finish_on_vector(b, some):
+            centre_and_gain(b, some)
+            scale_shift_store(b, some)
+
+        def finish_tile_on_vector(b, tiles):
+            for j in tiles:
+                nc.vector.scalar_tensor_tensor(
+                    out=out_sb[b][:, j, :],
+                    in0=o_sb[b][:, j, :],
+                    scalar=neg_mean[b][:],
+                    in1=gamma_sb[:, j, :],
+                    op0=ALU.add,
+                    op1=ALU.mult,
+                )
+            for j in tiles:
+                nc.vector.scalar_tensor_tensor(
+                    out=out_sb[b][:, j, :],
+                    in0=out_sb[b][:, j, :],
+                    scalar=rstd[b][:],
+                    in1=beta_sb[:, j, :],
+                    op0=ALU.mult,
+                    op1=ALU.add,
+                )
+                nc.sync.dma_start(out=out_view[b, :, j, :], in_=out_sb[b][:, j, :])
 
         def normalise(b, some):
             for chunk in some:
@@ -398,72 +427,69 @@ def tile_multiheadattn_pb_kernel(tc, h_attn, Wo, bo, x, gamma, beta, out):
                 )
                 nc.sync.dma_start(out=out_view[b, :, j, cols], in_=out_sb[b][:, j, cols])
 
-        for n in range(N_BLOCKS):
-            for g in range(PASSES):
+        for g in range(PASSES):
+            for n in range(N_BLOCKS):
+                group_wo(g, n)
+            for n in range(N_BLOCKS):
                 quantise_wo(g, n)
         for j in range(TILES):
             turn_h(0, j)
             group_h(nc.scalar.copy, 0, j)
             quantise_h(0, j)
+        for j in range(TILES):
+            turn_h(1, j)
+            group_h(nc.vector.tensor_copy if j == 1 else nc.scalar.copy, 1, j)
+            if j:
+                quantise_h(1, j - 1)
+        quantise_h(1, 3)
 
-        multiply(0, [0, 1])
+        multiply(0, [0])
         add_on_tensor(0, [0, 1])
         bring_out(0, [0, 1])
         add_on(nc.gpsimd, 0, [2, 3])
+        multiply(0, [1])
         multiply(0, [2, 3])
-        collect(0, [0, 1, 2])
         add_on_tensor(0, [4])
+        collect(0, [0, 1, 2, 3])
         square(0, [0])
         bring_out(0, [4])
-        square(0, [1, 2])
+        square(0, [1, 2, 3])
         add_on(nc.gpsimd, 0, [5, 6, 7])
-        multiply(0, [4, 5, 6])
-        collect(0, [3])
-        multiply(0, [7])
-        square(0, [3])
-        for j in range(TILES):
-            turn_h(1, j)
-            group_h(nc.scalar.copy, 1, j)
-            if j == 0:
-                collect(0, [4, 5, 6])
-        quantise_h(1, 0)
-        quantise_h(1, 1)
-        collect(0, [7])
-        quantise_h(1, 2)
-        quantise_h(1, 3)
-        multiply(1, [0])
+        multiply(0, [4, 5, 6, 7])
+        collect(0, [4, 5, 6, 7])
         add_on_tensor(1, [0])
         bring_out(1, [0])
+        square(0, [4, 5])
         add_on(nc.gpsimd, 1, [1, 2, 3])
-        multiply(1, [1, 2, 3])
-        square(0, [4, 5, 6])
-        add_on_tensor(1, [4, 5])
+        multiply(1, [0, 1])
+        add_on_tensor(1, [4])
+        multiply(1, [2])
+        add_on_tensor(1, [5])
+        multiply(1, [3])
+        collect(1, [0, 1, 2, 3])
+        square(0, [6])
         bring_out(1, [4, 5])
         square(0, [7])
-        collect(1, [0, 1, 2, 3])
         add_on(nc.gpsimd, 1, [6, 7])
-        multiply(1, [4])
+        multiply(1, [4, 5])
         add_sums_over_partitions(0)
-        multiply(1, [5, 6])
         find_mean(0)
-        square(1, [0, 1])
+        square(1, [0])
+        multiply(1, [6])
         add_squares_over_partitions(0)
         find_std(0)
         multiply(1, [7])
-        collect(1, [4, 5, 6])
+        collect(1, [4, 5, 6, 7])
+        square(1, [1])
         find_rstd(0)
-        collect(1, [7])
         square(1, [2, 3, 4, 5, 6, 7])
-        finish_on_vector(0, [0, 1])
-        finish_on_vector(0, [2, 3])
+        finish_tile_on_vector(0, [0, 1])
         add_sums_over_partitions(1)
         find_mean(1)
         add_squares_over_partitions(1)
         find_std(1)
-        finish_on_vector(0, [4, 5])
-        finish_on_vector(0, [6, 7])
+        finish_tile_on_vector(0, [2, 3])
         find_rstd(1)
-        finish_on_vector(1, [0, 1])
-        finish_on_vector(1, [2, 3])
-        finish_on_vector(1, [4, 5])
+        finish_tile_on_vector(1, [0, 1])
+        finish_tile_on_vector(1, [2])
         finish_on_vector(1, [6, 7])

@@ -313,6 +313,8 @@ def tile_multiheadattn_pb_kernel(tc, h_attn, Wo, bo, x, gamma, beta, out):
 
         def find_rstd(b):
             nc.vector.reciprocal(out=rstd[b][:], in_=std[b][:])
+
+        def find_shift(b):
             nc.scalar.activation(
                 out=shift[b][:], in_=neg_mean[b][:], func=ACT.Copy, scale=rstd[b][:]
             )
@@ -482,14 +484,38 @@ def tile_multiheadattn_pb_kernel(tc, h_attn, Wo, bo, x, gamma, beta, out):
         collect(1, [4, 5, 6, 7])
         square(1, [1])
         find_rstd(0)
+        for name, j in (("gamma", 2), ("gamma", 3)):
+            turn(name, j)
         square(1, [2, 3, 4, 5, 6, 7])
         finish_tile_on_vector(0, [0, 1])
         add_sums_over_partitions(1)
         find_mean(1)
         add_squares_over_partitions(1)
+        copy_turned("gamma", 2)
+        turn_back("gamma", 2)
         find_std(1)
-        finish_tile_on_vector(0, [2, 3])
         find_rstd(1)
-        finish_tile_on_vector(1, [0, 1])
-        finish_tile_on_vector(1, [2])
-        finish_on_vector(1, [6, 7])
+        find_shift(1)
+        normalise(1, [4, 5])
+        copy_turned("gamma", 3)
+        turn_back("gamma", 3)
+        normalise(1, [6])
+        turn("gamma", 0)
+        copy_turned("gamma", 0)
+        turn_back("gamma", 0)
+        normalise(1, [7])
+        turn("gamma", 1)
+        copy_turned("gamma", 1)
+        turn_back("gamma", 1)
+        normalise(1, [2])
+        finish_on_vector(0, [4])
+
+        shared = ((1, 4), (1, 5), (1, 6), (1, 7), (1, 2))
+        own = ((0, 5), (0, 6), (0, 7), (1, 0), (1, 1))
+        finish_on_gpsimd(shared[0][0], [shared[0][1]])
+        for i in range(len(own)):
+            centre_and_gain(own[i][0], [own[i][1]])
+            if i + 1 < len(shared):
+                finish_on_gpsimd(shared[i + 1][0], [shared[i + 1][1]])
+            scale_shift_store(own[i][0], [own[i][1]])
+        finish_on_vector(1, [3])

@@ -84,10 +84,10 @@ def tile_multiheadattn_pb_kernel(tc, h_attn, Wo, bo, x, gamma, beta, out):
                 in_=Wo[K_PASS * g : K_PASS * (g + 1), :].rearrange("(q t) c -> q t c", t=PACK),
             )
 
-        for g in range(PASSES):
-            load_wo(g)
         load_half([(h_raw[0], h_view[0])], 0)
         load_half([(h_raw[0], h_view[0])], 2)
+        for g in range(PASSES):
+            load_wo(g)
         load_half([(h_raw[1], h_view[1])], 0)
         load_half([(h_raw[1], h_view[1])], 2)
         load_half([(bo_sb[0], bo_view[0]), (x_sb[0], x_view[0])], 0)
@@ -429,27 +429,37 @@ def tile_multiheadattn_pb_kernel(tc, h_attn, Wo, bo, x, gamma, beta, out):
                 )
                 nc.sync.dma_start(out=out_view[b, :, j, cols], in_=out_sb[b][:, j, cols])
 
-        for g in range(PASSES):
-            for n in range(N_BLOCKS):
-                group_wo(g, n)
-            for n in range(N_BLOCKS):
-                quantise_wo(g, n)
-        for j in range(TILES):
+        for j in range(2):
+            turn_h(0, j)
+        group_h(nc.scalar.copy, 0, 0)
+        quantise_h(0, 0)
+        group_h(nc.vector.tensor_copy, 0, 1)
+        quantise_h(0, 1)
+        for j in range(2, TILES):
             turn_h(0, j)
             group_h(nc.scalar.copy, 0, j)
+        for n in range(N_BLOCKS):
+            group_wo(0, n)
+        for j in range(2, TILES):
             quantise_h(0, j)
+        for n in range(N_BLOCKS):
+            quantise_wo(0, n)
+        for n in range(N_BLOCKS):
+            group_wo(1, n)
+        for n in range(N_BLOCKS):
+            quantise_wo(1, n)
         for j in range(TILES):
             turn_h(1, j)
-            group_h(nc.vector.tensor_copy if j == 1 else nc.scalar.copy, 1, j)
-            if j:
-                quantise_h(1, j - 1)
-        quantise_h(1, 3)
+            group_h(nc.scalar.copy, 1, j)
+            quantise_h(1, j)
 
+        add_on_tensor(0, [0])
         multiply(0, [0])
-        add_on_tensor(0, [0, 1])
-        bring_out(0, [0, 1])
-        add_on(nc.gpsimd, 0, [2, 3])
+        bring_out(0, [0])
+        add_on_tensor(0, [1])
         multiply(0, [1])
+        bring_out(0, [1])
+        add_on(nc.gpsimd, 0, [2, 3])
         multiply(0, [2, 3])
         add_on_tensor(0, [4])
         collect(0, [0, 1, 2, 3])
@@ -484,38 +494,42 @@ def tile_multiheadattn_pb_kernel(tc, h_attn, Wo, bo, x, gamma, beta, out):
         collect(1, [4, 5, 6, 7])
         square(1, [1])
         find_rstd(0)
-        for name, j in (("gamma", 2), ("gamma", 3)):
-            turn(name, j)
+        for j in (2, 3, 0):
+            turn("gamma", j)
         square(1, [2, 3, 4, 5, 6, 7])
         finish_tile_on_vector(0, [0, 1])
         add_sums_over_partitions(1)
         find_mean(1)
-        add_squares_over_partitions(1)
         copy_turned("gamma", 2)
+        add_squares_over_partitions(1)
+        centre_and_gain(0, [4])
         turn_back("gamma", 2)
         find_std(1)
         find_rstd(1)
+        scale_shift_store(0, [4])
+        centre_and_gain(0, [5])
         find_shift(1)
-        normalise(1, [4, 5])
+        normalise(1, [4])
         copy_turned("gamma", 3)
+        normalise(1, [5])
         turn_back("gamma", 3)
-        normalise(1, [6])
-        turn("gamma", 0)
         copy_turned("gamma", 0)
-        turn_back("gamma", 0)
-        normalise(1, [7])
         turn("gamma", 1)
+        turn_back("gamma", 0)
+        normalise(1, [6])
         copy_turned("gamma", 1)
         turn_back("gamma", 1)
-        normalise(1, [2])
-        finish_on_vector(0, [4])
+        normalise(1, [7, 2])
 
         shared = ((1, 4), (1, 5), (1, 6), (1, 7), (1, 2))
         own = ((0, 5), (0, 6), (0, 7), (1, 0), (1, 1))
         finish_on_gpsimd(shared[0][0], [shared[0][1]])
         for i in range(len(own)):
-            centre_and_gain(own[i][0], [own[i][1]])
+            if i > 0:
+                centre_and_gain(own[i][0], [own[i][1]])
             if i + 1 < len(shared):
                 finish_on_gpsimd(shared[i + 1][0], [shared[i + 1][1]])
+            else:
+                centre_and_gain(1, [3])
             scale_shift_store(own[i][0], [own[i][1]])
-        finish_on_vector(1, [3])
+        scale_shift_store(1, [3])

@@ -202,6 +202,11 @@ def tile_multiheadattn_pb_kernel(tc, h_attn, Wo, bo, x, gamma, beta, out):
                     op=ALU.add,
                 )
 
+        def add_tile_on_gpsimd(b, j):
+            nc.gpsimd.tensor_tensor(
+                out=o_sb[b][:, j, :], in0=bo_sb[b][:, j, :], in1=x_sb[b][:, j, :], op=ALU.add
+            )
+
         boths = {}
 
         def add_on_tensor(b, some):
@@ -451,39 +456,47 @@ def tile_multiheadattn_pb_kernel(tc, h_attn, Wo, bo, x, gamma, beta, out):
         for j in range(TILES):
             turn_h(1, j)
             group_h(nc.scalar.copy, 1, j)
+        for j in range(3):
             quantise_h(1, j)
+        add_on(nc.vector, 0, [2])
+        quantise_h(1, 3)
+        nc.vector.memset(o_sb[0][:, 1, N - 1 : N], 0.0)
 
+        multiply(0, [2])
         add_on_tensor(0, [0])
-        multiply(0, [0])
         bring_out(0, [0])
+        multiply(0, [0])
         add_on_tensor(0, [1])
-        multiply(0, [1])
         bring_out(0, [1])
-        add_on(nc.gpsimd, 0, [2, 3])
-        multiply(0, [2, 3])
+        multiply(0, [1, 3])
+        add_on(nc.gpsimd, 0, [3])
         add_on_tensor(0, [4])
-        collect(0, [0, 1, 2, 3])
-        square(0, [0])
+        collect(0, [2, 0, 1, 3])
+        square(0, [2])
         bring_out(0, [4])
-        square(0, [1, 2, 3])
-        add_on(nc.gpsimd, 0, [5, 6, 7])
+        square(0, [0, 1])
+        add_on(nc.vector, 0, [5])
+        add_tile_on_gpsimd(0, 3)
         multiply(0, [4, 5, 6, 7])
         collect(0, [4, 5, 6, 7])
         add_on_tensor(1, [0])
+        square(0, [3])
         bring_out(1, [0])
         square(0, [4, 5])
-        add_on(nc.gpsimd, 1, [1, 2, 3])
+        add_on(nc.gpsimd, 1, [1])
+        add_tile_on_gpsimd(1, 1)
         multiply(1, [0, 1])
         add_on_tensor(1, [4])
         multiply(1, [2])
         add_on_tensor(1, [5])
         multiply(1, [3])
-        collect(1, [0, 1, 2, 3])
+        collect(1, [0, 1])
         square(0, [6])
         bring_out(1, [4, 5])
-        square(0, [7])
-        add_on(nc.gpsimd, 1, [6, 7])
         multiply(1, [4, 5])
+        collect(1, [2, 3, 4, 5])
+        square(0, [7])
+        add_tile_on_gpsimd(1, 3)
         add_sums_over_partitions(0)
         find_mean(0)
         square(1, [0])
@@ -491,7 +504,7 @@ def tile_multiheadattn_pb_kernel(tc, h_attn, Wo, bo, x, gamma, beta, out):
         add_squares_over_partitions(0)
         find_std(0)
         multiply(1, [7])
-        collect(1, [4, 5, 6, 7])
+        collect(1, [6, 7])
         square(1, [1])
         find_rstd(0)
         for j in (2, 3, 0):

@@ -188,6 +188,19 @@ def tile_multiheadattn_pb_kernel(tc, h_attn, Wo, bo, x, gamma, beta, out):
                 in_=h_grouped[b, j][:].rearrange("p g r t -> p (g r t)"),
             )
 
+        def keep_tensor_busy(passes):
+            unread_sums = psum_stat.tile([P, PASSES * P], F32, name="unread_sums", tag="stat")
+            for i in range(passes):
+                nc.tensor.matmul_mx(
+                    out=unread_sums[:],
+                    lhsT=h_codes[0][0][:, 0:P].bitcast(FP8X4),
+                    lhsT_scale=h_scales[0][0][:, 0:P],
+                    rhs=h_codes[0][0][:].bitcast(FP8X4),
+                    rhs_scale=h_scales[0][0][:],
+                    start=True,
+                    stop=True,
+                )
+
         def place(chunk):
             j, n = divmod(chunk, N_BLOCKS)
             return j, slice(N_BLOCK * n, N_BLOCK * (n + 1))
@@ -453,9 +466,12 @@ def tile_multiheadattn_pb_kernel(tc, h_attn, Wo, bo, x, gamma, beta, out):
             group_wo(1, n)
         for n in range(N_BLOCKS):
             quantise_wo(1, n)
+        keep_tensor_busy(20)
         for j in range(TILES):
             turn_h(1, j)
             group_h(nc.scalar.copy, 1, j)
+            if j % 2:
+                keep_tensor_busy(3)
         for j in range(3):
             quantise_h(1, j)
         add_on(nc.vector, 0, [2])
@@ -475,7 +491,7 @@ def tile_multiheadattn_pb_kernel(tc, h_attn, Wo, bo, x, gamma, beta, out):
         square(0, [2])
         bring_out(0, [4])
         square(0, [0, 1])
-        add_on(nc.vector, 0, [5])
+        add_on(nc.gpsimd, 0, [5])
         add_tile_on_gpsimd(0, 3)
         multiply(0, [4, 5, 6, 7])
         collect(0, [4, 5, 6, 7])

@@ -215,8 +215,8 @@ def tile_multiheadattn_pb_kernel(tc, h_attn, Wo, bo, x, gamma, beta, out):
                     op=ALU.add,
                 )
 
-        def add_tile_on_gpsimd(b, j):
-            nc.gpsimd.tensor_tensor(
+        def add_tile(engine, b, j):
+            engine.tensor_tensor(
                 out=o_sb[b][:, j, :], in0=bo_sb[b][:, j, :], in1=x_sb[b][:, j, :], op=ALU.add
             )
 
@@ -398,26 +398,32 @@ def tile_multiheadattn_pb_kernel(tc, h_attn, Wo, bo, x, gamma, beta, out):
             centre_and_gain(b, some)
             scale_shift_store(b, some)
 
+        def centre_tile(b, j):
+            nc.vector.scalar_tensor_tensor(
+                out=out_sb[b][:, j, :],
+                in0=o_sb[b][:, j, :],
+                scalar=neg_mean[b][:],
+                in1=gamma_sb[:, j, :],
+                op0=ALU.add,
+                op1=ALU.mult,
+            )
+
+        def scale_shift_store_tile(b, j):
+            nc.vector.scalar_tensor_tensor(
+                out=out_sb[b][:, j, :],
+                in0=out_sb[b][:, j, :],
+                scalar=rstd[b][:],
+                in1=beta_sb[:, j, :],
+                op0=ALU.mult,
+                op1=ALU.add,
+            )
+            nc.sync.dma_start(out=out_view[b, :, j, :], in_=out_sb[b][:, j, :])
+
         def finish_tile_on_vector(b, tiles):
             for j in tiles:
-                nc.vector.scalar_tensor_tensor(
-                    out=out_sb[b][:, j, :],
-                    in0=o_sb[b][:, j, :],
-                    scalar=neg_mean[b][:],
-                    in1=gamma_sb[:, j, :],
-                    op0=ALU.add,
-                    op1=ALU.mult,
-                )
+                centre_tile(b, j)
             for j in tiles:
-                nc.vector.scalar_tensor_tensor(
-                    out=out_sb[b][:, j, :],
-                    in0=out_sb[b][:, j, :],
-                    scalar=rstd[b][:],
-                    in1=beta_sb[:, j, :],
-                    op0=ALU.mult,
-                    op1=ALU.add,
-                )
-                nc.sync.dma_start(out=out_view[b, :, j, :], in_=out_sb[b][:, j, :])
+                scale_shift_store_tile(b, j)
 
         def normalise(b, some):
             for chunk in some:
@@ -474,45 +480,45 @@ def tile_multiheadattn_pb_kernel(tc, h_attn, Wo, bo, x, gamma, beta, out):
                 keep_tensor_busy(3)
         for j in range(3):
             quantise_h(1, j)
-        add_on(nc.vector, 0, [2])
+        add_tile(nc.vector, 0, 1)
         quantise_h(1, 3)
-        nc.vector.memset(o_sb[0][:, 1, N - 1 : N], 0.0)
 
-        multiply(0, [2])
+        multiply(0, [2, 3])
         add_on_tensor(0, [0])
         bring_out(0, [0])
         multiply(0, [0])
         add_on_tensor(0, [1])
         bring_out(0, [1])
-        multiply(0, [1, 3])
-        add_on(nc.gpsimd, 0, [3])
+        multiply(0, [1])
         add_on_tensor(0, [4])
-        collect(0, [2, 0, 1, 3])
+        collect(0, [2, 3, 0, 1])
         square(0, [2])
         bring_out(0, [4])
-        square(0, [0, 1])
+        square(0, [3, 0])
         add_on(nc.gpsimd, 0, [5])
-        add_tile_on_gpsimd(0, 3)
+        add_tile(nc.gpsimd, 0, 3)
         multiply(0, [4, 5, 6, 7])
         collect(0, [4, 5, 6, 7])
         add_on_tensor(1, [0])
-        square(0, [3])
+        square(0, [1])
         bring_out(1, [0])
-        square(0, [4, 5])
+        square(0, [4])
         add_on(nc.gpsimd, 1, [1])
-        add_tile_on_gpsimd(1, 1)
+        add_tile(nc.gpsimd, 1, 1)
         multiply(1, [0, 1])
         add_on_tensor(1, [4])
-        multiply(1, [2])
+        multiply(1, [4])
         add_on_tensor(1, [5])
-        multiply(1, [3])
+        multiply(1, [5])
         collect(1, [0, 1])
+        bring_out(1, [4])
+        square(0, [5])
+        bring_out(1, [5])
         square(0, [6])
-        bring_out(1, [4, 5])
-        multiply(1, [4, 5])
-        collect(1, [2, 3, 4, 5])
+        multiply(1, [2, 3])
+        collect(1, [4, 5, 2, 3])
         square(0, [7])
-        add_tile_on_gpsimd(1, 3)
+        add_on(nc.gpsimd, 1, [6, 7])
         add_sums_over_partitions(0)
         find_mean(0)
         square(1, [0])
@@ -538,9 +544,8 @@ def tile_multiheadattn_pb_kernel(tc, h_attn, Wo, bo, x, gamma, beta, out):
         scale_shift_store(0, [4])
         centre_and_gain(0, [5])
         find_shift(1)
-        normalise(1, [4])
+        normalise(1, [4, 5])
         copy_turned("gamma", 3)
-        normalise(1, [5])
         turn_back("gamma", 3)
         copy_turned("gamma", 0)
         turn("gamma", 1)

@@ -188,19 +188,6 @@ def tile_multiheadattn_pb_kernel(tc, h_attn, Wo, bo, x, gamma, beta, out):
                 in_=h_grouped[b, j][:].rearrange("p g r t -> p (g r t)"),
             )
 
-        def keep_tensor_busy(passes):
-            unread_sums = psum_stat.tile([P, PASSES * P], F32, name="unread_sums", tag="stat")
-            for i in range(passes):
-                nc.tensor.matmul_mx(
-                    out=unread_sums[:],
-                    lhsT=h_codes[0][0][:, 0:P].bitcast(FP8X4),
-                    lhsT_scale=h_scales[0][0][:, 0:P],
-                    rhs=h_codes[0][0][:].bitcast(FP8X4),
-                    rhs_scale=h_scales[0][0][:],
-                    start=True,
-                    stop=True,
-                )
-
         def place(chunk):
             j, n = divmod(chunk, N_BLOCKS)
             return j, slice(N_BLOCK * n, N_BLOCK * (n + 1))
@@ -472,12 +459,9 @@ def tile_multiheadattn_pb_kernel(tc, h_attn, Wo, bo, x, gamma, beta, out):
             group_wo(1, n)
         for n in range(N_BLOCKS):
             quantise_wo(1, n)
-        keep_tensor_busy(20)
         for j in range(TILES):
             turn_h(1, j)
             group_h(nc.scalar.copy, 1, j)
-            if j % 2:
-                keep_tensor_busy(3)
         for j in range(3):
             quantise_h(1, j)
         add_tile(nc.vector, 0, 1)

from contextlib import ExitStack

import concourse.mybir as mybir
from concourse.masks import make_identity

F32 = mybir.dt.float32
BF16 = mybir.dt.bfloat16
U32 = mybir.dt.uint32
U8 = mybir.dt.uint8
FP8X4 = mybir.dt.float8_e4m3fn_x4
ALU = mybir.AluOpType
ACT = mybir.ActivationFunctionType

P = 128
BATCH = 2
SEQ = 512
K = 1024
N = 1024
LN_EPS = 1e-5

PACK = 4
K_PASS = P * PACK
PASSES = K // K_PASS
HALVES = 2
N_BLOCK = 512
N_BLOCKS = N // N_BLOCK
TILES = SEQ // P
RUN = 4

VECTOR_COLS = 336

FLOPS = 2 * BATCH * SEQ * K * N


def tile_multiheadattn_pb_kernel(tc, h_attn, Wo, bo, x, gamma, beta, out):
    nc = tc.nc
    with ExitStack() as ctx:
        const = ctx.enter_context(tc.tile_pool(name="const", bufs=1))
        keep = ctx.enter_context(tc.tile_pool(name="keep", bufs=1))
        scratch = ctx.enter_context(tc.tile_pool(name="scratch", bufs=2))
        psum_work = ctx.enter_context(tc.psum_pool(name="psum_work", bufs=3))
        psum_acc = ctx.enter_context(tc.psum_pool(name="psum_acc", bufs=4))
        psum_stat = ctx.enter_context(tc.psum_pool(name="psum_stat", bufs=1))
        ctx.enter_context(tc.manual_schedule())

        ident = const.tile([P, P], F32)
        make_identity(nc, ident[:])
        ident16 = const.tile([P, P], BF16)
        make_identity(nc, ident16[:])
        mean_w = const.tile([P, P], F32)
        nc.vector.memset(mean_w[:], 1.0 / (SEQ * N))
        within_w = const.tile([P, P], F32)
        nc.vector.memset(within_w[:], 1.0 / (SEQ * N * N_BLOCK * N_BLOCK))
        between_w = const.tile([P, P], F32)
        nc.vector.memset(between_w[:], N_BLOCK / (SEQ * N))
        eps = const.tile([P, 1], F32)
        nc.vector.memset(eps[:], LN_EPS)
        warm = const.tile([P, 1], F32)
        nc.scalar.activation(out=warm[:], in_=eps[:], func=ACT.Sqrt)

        h_view = h_attn.rearrange("b (p j) k -> b p j k", j=TILES)
        bo_view = bo.rearrange("b (p j) n -> b p j n", j=TILES)
        x_view = x.rearrange("b (p j) n -> b p j n", j=TILES)
        gamma_view = gamma.rearrange("(p j) n -> p j n", j=TILES)
        beta_view = beta.rearrange("(p j) n -> p j n", j=TILES)
        out_view = out.rearrange("b (p j) n -> b p j n", j=TILES)

        wo_raw = [
            keep.tile([P, PACK, N], BF16, name="wo_raw%d" % g) for g in range(PASSES)
        ]
        h_raw = [keep.tile([P, TILES, K], BF16, name="h_raw%d" % b) for b in range(BATCH)]
        bo_sb = [keep.tile([P, TILES, N], BF16, name="bo_sb%d" % b) for b in range(BATCH)]
        x_sb = [keep.tile([P, TILES, N], BF16, name="x_sb%d" % b) for b in range(BATCH)]
        gamma_sb = keep.tile([P, TILES, N], BF16)
        beta_sb = keep.tile([P, TILES, N], BF16)

        def load_half(pairs, first):
            for dst, src in pairs:
                nc.sync.dma_start(out=dst[:, first : first + 2, :], in_=src[:, first : first + 2, :])

        def load_wo(g):
            nc.sync.dma_start(
                out=wo_raw[g][:],
                in_=Wo[K_PASS * g : K_PASS * (g + 1), :].rearrange("(q t) c -> q t c", t=PACK),
            )

        load_half([(h_raw[0], h_view[0])], 0)
        load_half([(h_raw[0], h_view[0])], 2)
        for g in range(PASSES):
            load_wo(g)
        load_half([(h_raw[1], h_view[1])], 0)
        load_half([(h_raw[1], h_view[1])], 2)
        load_half([(bo_sb[0], bo_view[0]), (x_sb[0], x_view[0])], 0)
        load_half([(bo_sb[0], bo_view[0]), (x_sb[0], x_view[0])], 2)
        load_half([(bo_sb[1], bo_view[1]), (x_sb[1], x_view[1])], 0)
        load_half([(bo_sb[1], bo_view[1]), (x_sb[1], x_view[1])], 2)
        nc.sync.dma_start(out=gamma_sb[:], in_=gamma_view)
        nc.sync.dma_start(out=beta_sb[:], in_=beta_view)

        wo_codes = [
            keep.tile([P, N], U32, name="wo_codes%d" % g, align_bytes=64) for g in range(PASSES)
        ]
        wo_scales = [
            keep.tile([P, N], U8, name="wo_scales%d" % g, align_bytes=64) for g in range(PASSES)
        ]
        o_sb = [keep.tile([P, TILES, N], F32, name="o_sb%d" % b) for b in range(BATCH)]
        out_sb = [keep.tile([P, TILES, N], F32, name="out_sb%d" % b) for b in range(BATCH)]
        h_codes = [
            [
                keep.tile([P, PASSES * P], U32, name="h_codes%d_%d" % (b, j), align_bytes=64)
                for j in range(TILES)
            ]
            for b in range(BATCH)
        ]
        h_scales = [
            [
                keep.tile([P, PASSES * P], U8, name="h_scales%d_%d" % (b, j), align_bytes=64)
                for j in range(TILES)
            ]
            for b in range(BATCH)
        ]
        chunk_sums = [
            keep.tile([P, TILES * N_BLOCKS], F32, name="chunk_sums%d" % b) for b in range(BATCH)
        ]
        within = [keep.tile([P, TILES * N_BLOCKS], F32, name="within%d" % b) for b in range(BATCH)]
        neg_mean = [keep.tile([P, 1], F32, name="neg_mean%d" % b) for b in range(BATCH)]
        std = [keep.tile([P, 1], F32, name="std%d" % b) for b in range(BATCH)]
        rstd = [keep.tile([P, 1], F32, name="rstd%d" % b) for b in range(BATCH)]
        shift = [keep.tile([P, 1], F32, name="shift%d" % b) for b in range(BATCH)]

        wo_grouped = {}

        def group_wo(g, n):
            grouped = keep.tile(
                [P, N_BLOCK, PACK], BF16, name="wo_grouped%d_%d" % (g, n), align_bytes=64
            )
            for copy, cols in (
                (nc.vector.tensor_copy, slice(0, VECTOR_COLS)),
                (nc.scalar.copy, slice(VECTOR_COLS, N_BLOCK)),
            ):
                first = N_BLOCK * n + cols.start
                copy(
                    out=grouped[:, cols, :].rearrange("p (c i) t -> p c t i", i=RUN),
                    in_=wo_raw[g][:, :, first : first + cols.stop - cols.start].rearrange(
                        "p t (c i) -> p c t i", i=RUN
                    ),
                )
            wo_grouped[g, n] = grouped

        def quantise_wo(g, n):
            cols = slice(N_BLOCK * n, N_BLOCK * (n + 1))
            nc.vector.quantize_mx(
                out=wo_codes[g][:, cols].bitcast(FP8X4),
                scales=wo_scales[g][:, cols],
                in_=wo_grouped[g, n][:].rearrange("p c t -> p (c t)"),
            )

        h_turned = {}
        h_grouped = {}

        def turn_h(b, j):
            words = h_raw[b][:, j, :].bitcast(F32)
            turned = psum_work.tile([P, PASSES, HALVES, P], F32, name="turned", tag="work")
            for g in range(PASSES):
                for u in range(HALVES):
                    first = HALVES * P * g
                    nc.tensor.transpose(
                        turned[:, g, u, :],
                        words[:, first + u : first + HALVES * P : HALVES],
                        ident[:],
                    )
            h_turned[b, j] = turned

        def group_h(copy, b, j):
            grouped = keep.tile(
                [P, PASSES, P, PACK], BF16, name="h_grouped%d_%d" % (b, j), align_bytes=64
            )
            copy(
                out=grouped[:].bitcast(F32),
                in_=h_turned[b, j][:].rearrange("p g u r -> p g r u"),
            )
            h_grouped[b, j] = grouped

        def quantise_h(b, j):
            nc.vector.quantize_mx(
                out=h_codes[b][j][:].bitcast(FP8X4),
                scales=h_scales[b][j][:],
                in_=h_grouped[b, j][:].rearrange("p g r t -> p (g r t)"),
            )

        def place(chunk):
            j, n = divmod(chunk, N_BLOCKS)
            return j, slice(N_BLOCK * n, N_BLOCK * (n + 1))

        def add_on(engine, b, some):
            for chunk in some:
                j, cols = place(chunk)
                engine.tensor_tensor(
                    out=o_sb[b][:, j, cols],
                    in0=bo_sb[b][:, j, cols],
                    in1=x_sb[b][:, j, cols],
                    op=ALU.add,
                )

        def add_tile(engine, b, j):
            engine.tensor_tensor(
                out=o_sb[b][:, j, :], in0=bo_sb[b][:, j, :], in1=x_sb[b][:, j, :], op=ALU.add
            )

        boths = {}

        def add_on_tensor(b, some):
            for chunk in some:
                j, cols = place(chunk)
                both = psum_work.tile([P, N_BLOCK], F32, name="both", tag="work")
                boths[b, chunk] = both
                nc.tensor.matmul(
                    out=both[:], lhsT=ident16[:], rhs=bo_sb[b][:, j, cols], start=True, stop=False
                )
                nc.tensor.matmul(
                    out=both[:], lhsT=ident16[:], rhs=x_sb[b][:, j, cols], start=False, stop=True
                )

        def bring_out(b, some):
            for chunk in some:
                j, cols = place(chunk)
                nc.scalar.copy(out=o_sb[b][:, j, cols], in_=boths[b, chunk][:])

        accs = {}

        def multiply(b, some):
            for chunk in some:
                j, cols = place(chunk)
                acc = psum_acc.tile([P, N_BLOCK], F32, name="acc")
                accs[b, chunk] = acc
                for g in range(PASSES):
                    tokens = slice(P * g, P * (g + 1))
                    nc.tensor.matmul_mx(
                        out=acc[:],
                        lhsT=h_codes[b][j][:, tokens].bitcast(FP8X4),
                        lhsT_scale=h_scales[b][j][:, tokens],
                        rhs=wo_codes[g][:, cols].bitcast(FP8X4),
                        rhs_scale=wo_scales[g][:, cols],
                        start=(g == 0),
                        stop=(g == PASSES - 1),
                    )

        def collect(b, some):
            for chunk in some:
                j, cols = place(chunk)
                nc.vector.scalar_tensor_tensor(
                    out=o_sb[b][:, j, cols],
                    in0=accs[b, chunk][:],
                    scalar=1.0,
                    in1=o_sb[b][:, j, cols],
                    op0=ALU.mult,
                    op1=ALU.add,
                    accum_out=chunk_sums[b][:, chunk : chunk + 1],
                )

        chunks = TILES * N_BLOCKS

        def square(b, some):
            for chunk in some:
                squares = scratch.tile([P, N_BLOCK], BF16, name="squares")
                j, cols = place(chunk)
                nc.scalar.activation(
                    out=squares[:],
                    in_=o_sb[b][:, j, cols],
                    func=ACT.Square,
                    bias=chunk_sums[b][:, chunk : chunk + 1],
                    scale=-float(N_BLOCK),
                    accum_out=within[b][:, chunk : chunk + 1],
                )

        chunk_means = {}
        parts = {}

        def add_sums_over_partitions(b):
            chunk_means[b] = psum_stat.tile([P, chunks], F32, name="chunk_means", tag="stat")
            nc.tensor.matmul(
                out=chunk_means[b][:], lhsT=mean_w[:], rhs=chunk_sums[b][:], start=True, stop=True
            )

        between = [keep.tile([P, chunks], F32, name="between%d" % b) for b in range(BATCH)]

        def find_mean(b):
            unread = scratch.tile([P, chunks], F32, name="unread")
            nc.scalar.activation(
                out=unread[:],
                in_=chunk_means[b][:],
                func=ACT.Copy,
                scale=-1.0,
                accum_out=neg_mean[b][:],
            )
            nc.scalar.activation(
                out=between[b][:],
                in_=chunk_sums[b][:],
                func=ACT.Square,
                bias=neg_mean[b][:],
                scale=1.0 / N_BLOCK,
            )

        def add_squares_over_partitions(b):
            parts[b] = psum_stat.tile([P, chunks], F32, name="parts", tag="stat")
            nc.tensor.matmul(
                out=parts[b][:], lhsT=within_w[:], rhs=within[b][:], start=True, stop=False
            )
            nc.tensor.matmul(
                out=parts[b][:], lhsT=between_w[:], rhs=between[b][:], start=False, stop=True
            )

        def find_std(b):
            unread = scratch.tile([P, chunks], F32, name="unread")
            var = scratch.tile([P, 1], F32, name="var")
            nc.scalar.activation(out=unread[:], in_=parts[b][:], func=ACT.Copy, accum_out=var[:])
            nc.scalar.activation(out=std[b][:], in_=var[:], func=ACT.Sqrt, bias=eps[:], scale=1.0)

        def find_rstd(b):
            nc.vector.reciprocal(out=rstd[b][:], in_=std[b][:])

        def find_shift(b):
            nc.scalar.activation(
                out=shift[b][:], in_=neg_mean[b][:], func=ACT.Copy, scale=rstd[b][:]
            )

        words = N_BLOCK // P
        in_sbuf = {"gamma": gamma_sb, "beta": beta_sb}
        in_psum = {}
        turned = {}
        turned_sb = {}

        def turn(name, j):
            turned[name, j] = psum_work.tile([P, words, P], F32, name="turned_once", tag="work")
            for w in range(words):
                nc.tensor.transpose(
                    turned[name, j][:, w, :],
                    in_sbuf[name][:, j, :].bitcast(F32)[:, P * w : P * (w + 1)],
                    ident[:],
                )

        def copy_turned(name, j):
            turned_sb[name, j] = keep.tile([P, words, P], F32, name="turned_%s%d" % (name, j))
            nc.scalar.copy(out=turned_sb[name, j][:], in_=turned[name, j][:])

        def turn_back(name, j, pool=psum_acc, tag="acc"):
            back = pool.tile([P, words, P], F32, name="turned_twice", tag=tag)
            for w in range(words):
                nc.tensor.transpose(back[:, w, :], turned_sb[name, j][:, w, :], ident[:])
            in_psum[name, j] = back

        def columns(name, chunk):
            j, cols = place(chunk)
            if (name, j) in in_psum:
                back = in_psum[name, j][:].rearrange("p w r -> p (w r)")
                return back.bitcast(BF16)[:, cols]
            return in_sbuf[name][:, j, cols]

        def centre_and_gain(b, some):
            for chunk in some:
                j, cols = place(chunk)
                nc.vector.scalar_tensor_tensor(
                    out=out_sb[b][:, j, cols],
                    in0=o_sb[b][:, j, cols],
                    scalar=neg_mean[b][:],
                    in1=columns("gamma", chunk),
                    op0=ALU.add,
                    op1=ALU.mult,
                )

        def scale_shift_store(b, some):
            for chunk in some:
                j, cols = place(chunk)
                nc.vector.scalar_tensor_tensor(
                    out=out_sb[b][:, j, cols],
                    in0=out_sb[b][:, j, cols],
                    scalar=rstd[b][:],
                    in1=columns("beta", chunk),
                    op0=ALU.mult,
                    op1=ALU.add,
                )
                nc.sync.dma_start(out=out_view[b, :, j, cols], in_=out_sb[b][:, j, cols])

        def finish_on_vector(b, some):
            centre_and_gain(b, some)
            scale_shift_store(b, some)

        def centre_tile(b, j):
            nc.vector.scalar_tensor_tensor(
                out=out_sb[b][:, j, :],
                in0=o_sb[b][:, j, :],
                scalar=neg_mean[b][:],
                in1=gamma_sb[:, j, :],
                op0=ALU.add,
                op1=ALU.mult,
            )

        def scale_shift_store_tile(b, j):
            nc.vector.scalar_tensor_tensor(
                out=out_sb[b][:, j, :],
                in0=out_sb[b][:, j, :],
                scalar=rstd[b][:],
                in1=beta_sb[:, j, :],
                op0=ALU.mult,
                op1=ALU.add,
            )
            nc.sync.dma_start(out=out_view[b, :, j, :], in_=out_sb[b][:, j, :])

        def finish_tile_on_vector(b, tiles):
            for j in tiles:
                centre_tile(b, j)
            for j in tiles:
                scale_shift_store_tile(b, j)

        def normalise(b, some):
            for chunk in some:
                j, cols = place(chunk)
                nc.scalar.activation(
                    out=out_sb[b][:, j, cols],
                    in_=o_sb[b][:, j, cols],
                    func=ACT.Identity,
                    bias=shift[b][:],
                    scale=rstd[b][:],
                )

        def finish_on_gpsimd(b, some):
            for chunk in some:
                j, cols = place(chunk)
                nc.vector.tensor_tensor(
                    out=out_sb[b][:, j, cols],
                    in0=out_sb[b][:, j, cols],
                    in1=columns("gamma", chunk),
                    op=ALU.mult,
                )
                nc.gpsimd.tensor_tensor(
                    out=out_sb[b][:, j, cols],
                    in0=out_sb[b][:, j, cols],
                    in1=beta_sb[:, j, cols],
                    op=ALU.add,
                )
                nc.sync.dma_start(out=out_view[b, :, j, cols], in_=out_sb[b][:, j, cols])

        for j in range(2):
            turn_h(0, j)
        group_h(nc.scalar.copy, 0, 0)
        quantise_h(0, 0)
        group_h(nc.vector.tensor_copy, 0, 1)
        quantise_h(0, 1)
        for j in range(2, TILES):
            turn_h(0, j)
            group_h(nc.scalar.copy, 0, j)
        for n in range(N_BLOCKS):
            group_wo(0, n)
        for j in range(2, TILES):
            quantise_h(0, j)
        for n in range(N_BLOCKS):
            quantise_wo(0, n)
        for n in range(N_BLOCKS):
            group_wo(1, n)
        for n in range(N_BLOCKS):
            quantise_wo(1, n)
        for j in range(TILES):
            turn_h(1, j)
            group_h(nc.scalar.copy, 1, j)
        for j in range(3):
            quantise_h(1, j)
        add_tile(nc.vector, 0, 1)
        quantise_h(1, 3)

        multiply(0, [2, 3])
        add_on_tensor(0, [0])
        bring_out(0, [0])
        multiply(0, [0])
        add_on_tensor(0, [1])
        bring_out(0, [1])
        multiply(0, [1])
        add_on_tensor(0, [4])
        collect(0, [2, 3, 0, 1])
        square(0, [2])
        bring_out(0, [4])
        square(0, [3, 0])
        add_on(nc.gpsimd, 0, [5])
        add_tile(nc.gpsimd, 0, 3)
        multiply(0, [4, 5, 6, 7])
        collect(0, [4, 5, 6, 7])
        add_on_tensor(1, [0])
        square(0, [1])
        bring_out(1, [0])
        square(0, [4])
        add_on(nc.gpsimd, 1, [1])
        add_tile(nc.gpsimd, 1, 1)
        multiply(1, [0, 1])
        add_on_tensor(1, [4])
        multiply(1, [4])
        add_on_tensor(1, [5])
        multiply(1, [5])
        collect(1, [0, 1])
        bring_out(1, [4])
        square(0, [5])
        bring_out(1, [5])
        square(0, [6])
        multiply(1, [2, 3])
        collect(1, [4, 5, 2, 3])
        square(0, [7])
        add_on(nc.gpsimd, 1, [6, 7])
        add_sums_over_partitions(0)
        find_mean(0)
        square(1, [0])
        multiply(1, [6])
        add_squares_over_partitions(0)
        find_std(0)
        multiply(1, [7])
        collect(1, [6, 7])
        square(1, [1])
        find_rstd(0)
        for j in (2, 3, 0):
            turn("gamma", j)
        square(1, [2, 3, 4, 5, 6, 7])
        finish_tile_on_vector(0, [0, 1])
        add_sums_over_partitions(1)
        find_mean(1)
        copy_turned("gamma", 2)
        add_squares_over_partitions(1)
        centre_and_gain(0, [4])
        turn_back("gamma", 2)
        find_std(1)
        find_rstd(1)
        scale_shift_store(0, [4])
        centre_and_gain(0, [5])
        find_shift(1)
        normalise(1, [4, 5])
        copy_turned("gamma", 3)
        turn_back("gamma", 3)
        copy_turned("gamma", 0)
        turn("gamma", 1)
        turn_back("gamma", 0)
        normalise(1, [6])
        copy_turned("gamma", 1)
        turn_back("gamma", 1)
        normalise(1, [7, 2])

        shared = ((1, 4), (1, 5), (1, 6), (1, 7), (1, 2))
        own = ((0, 5), (0, 6), (0, 7), (1, 0), (1, 1))
        finish_on_gpsimd(shared[0][0], [shared[0][1]])
        for i in range(len(own)):
            if i > 0:
                centre_and_gain(own[i][0], [own[i][1]])
            if i + 1 < len(shared):
                finish_on_gpsimd(shared[i + 1][0], [shared[i + 1][1]])
            else:
                centre_and_gain(1, [3])
            scale_shift_store(own[i][0], [own[i][1]])
        scale_shift_store(1, [3])
